import numpy as np
import ml_dtypes

BF16 = ml_dtypes.bfloat16


def bf(x):
    return np.asarray(x, np.float32).astype(BF16)


def f32(x):
    return np.asarray(x, np.float32)


def f64(x):
    return np.asarray(x).astype(np.float64)


def striped(idx):
    return np.tile(idx.reshape(-1, 16).T, (8, 1))


S, N, BLK, R, NB, C, F = 1024, 128, 128, 4, 4, 512, 512


def setup_inputs():
    return {"xt": f32(np.random.standard_normal((F, N))), "rule_in": f32(np.random.standard_normal((C, S)) / np.sqrt(BLK)), "rule_out_tok": f32(np.random.standard_normal((C, N)) / np.sqrt(R)), "logits_tok": f32(np.random.standard_normal((NB, N)) / np.sqrt(NB)), "offs": striped(np.random.permutation(S)[:N])}


def reference(xt, rule_in, rule_out_tok, logits_tok, offs):
    idx = offs[:16].T.reshape(-1)
    rin = f64(rule_in)[:, idx].reshape(R, BLK, N)
    xb = f64(xt).reshape(NB, BLK, N)
    hidden = np.einsum('ksj,rsj->krj', xb, rin)
    adapter = np.einsum('krj,rtj->ktj', hidden, f64(rule_out_tok).reshape(R, BLK, N))
    e = np.exp(f64(logits_tok) * np.sqrt(NB))
    sel = e / e.sum(axis=0, keepdims=True)
    return (adapter * sel[:, None, :]).reshape(F, N)

@@ -1,0 +1,103 @@
+import concourse.mybir as mybir
+
+F32, BF16, U16 = mybir.dt.float32, mybir.dt.bfloat16, mybir.dt.uint16
+MULT, ADD, SUBTRACT, MAX = (
+    mybir.AluOpType.mult,
+    mybir.AluOpType.add,
+    mybir.AluOpType.subtract,
+    mybir.AluOpType.max,
+)
+EXP, COPY = mybir.ActivationFunctionType.Exp, mybir.ActivationFunctionType.Copy
+
+P = 128
+TOKENS = 128
+RULES = 1024
+RANKS = 4
+BLOCKS = 4
+WIDE = BLOCKS * TOKENS
+
+FLOPS = 2 * (2 * BLOCKS * RANKS * P * TOKENS)
+
+
+def by_block(ap):
+    return ap.rearrange("p (k j) -> p k j", k=BLOCKS)
+
+
+def over_blocks(ap):
+    return ap.unsqueeze(1).to_broadcast([P, BLOCKS, TOKENS])
+
+
+def tile_ruleawareprojection_kernel(tc, xt, rule_in, rule_out_tok, logits_tok, offs, out):
+    nc = tc.nc
+    with (
+        tc.tile_pool(name="held", bufs=1) as held,
+        tc.tile_pool(name="ring", bufs=2) as ring,
+        tc.psum_pool(name="psum", bufs=2) as psum,
+    ):
+        offsets = held.tile([P, TOKENS // 16], U16, name="offsets")
+        nc.sync.dma_start(offsets[:], offs)
+        tables = []
+        for r in range(RANKS):
+            table = held.tile([P, RULES], F32, name=f"table{r}")
+            nc.sync.dma_start(table[:], rule_in[r * P : (r + 1) * P, :])
+            tables.append(table)
+
+        x = held.tile([P, WIDE], F32, name="x")
+        nc.scalar.dma_start(by_block(x[:]), xt.rearrange("(k s) j -> s k j", s=P))
+        logits = held.tile([P, WIDE], F32, name="logits")
+        nc.scalar.dma_start(logits[:], logits_tok.rearrange("k j -> (k j)").partition_broadcast(P))
+        factor_out = held.tile([P, RANKS * TOKENS], F32, name="factor_out")
+        nc.scalar.dma_start(
+            factor_out[:].rearrange("t (r j) -> t r j", r=RANKS),
+            rule_out_tok.rearrange("(r t) j -> t r j", t=P),
+        )
+
+        ones = held.tile([P, P], BF16, name="ones")
+        nc.gpsimd.memset(ones[:], 1.0)
+
+        half = held.tile([P, 2 * TOKENS], F32, name="half")
+        nc.vector.tensor_tensor(half[:], logits[:, : 2 * TOKENS], logits[:, 2 * TOKENS :], MAX)
+        peak = held.tile([P, TOKENS], F32, name="peak")
+        nc.vector.tensor_tensor(peak[:], half[:, :TOKENS], half[:, TOKENS:], MAX)
+        shifted = held.tile([P, WIDE], F32, name="shifted")
+        nc.vector.tensor_tensor(by_block(shifted[:]), by_block(logits[:]), over_blocks(peak[:]), SUBTRACT)
+        weight = held.tile([P, WIDE], F32, name="weight")
+        nc.scalar.activation(weight[:], shifted[:], EXP, scale=2.0)
+        half_sum = held.tile([P, 2 * TOKENS], F32, name="half_sum")
+        nc.vector.tensor_tensor(half_sum[:], weight[:, : 2 * TOKENS], weight[:, 2 * TOKENS :], ADD)
+        total = held.tile([P, TOKENS], F32, name="total")
+        nc.vector.tensor_tensor(total[:], half_sum[:, :TOKENS], half_sum[:, TOKENS:], ADD)
+        inverse = held.tile([P, TOKENS], F32, name="inverse")
+        nc.vector.reciprocal(inverse[:], total[:])
+        sel = held.tile([P, WIDE], F32, name="sel")
+        nc.vector.tensor_tensor(by_block(sel[:]), by_block(weight[:]), over_blocks(inverse[:]), MULT)
+
+        adapter = None
+        for r in range(RANKS):
+            product = ring.tile([P, WIDE], F32, name="product")
+            for k in range(BLOCKS):
+                cols = slice(k * TOKENS, (k + 1) * TOKENS)
+                nc.vector.tensor_tensor(product[:, cols], tables[r][:].indirect(offsets[:]), x[:, cols], MULT)
+            rounded = ring.tile([P, WIDE], BF16, name="rounded")
+            nc.scalar.activation(rounded[:], product[:], COPY)
+
+            hidden = psum.tile([P, WIDE], F32, name="hidden")
+            nc.tensor.matmul(hidden[:], ones[:], rounded[:])
+
+            term = held.tile([P, WIDE], F32, name=f"term{r}")
+            nc.vector.tensor_tensor(
+                by_block(term[:]),
+                by_block(hidden[:]),
+                over_blocks(factor_out[:, r * TOKENS : (r + 1) * TOKENS]),
+                MULT,
+            )
+            if adapter is None:
+                adapter = term
+            else:
+                summed = held.tile([P, WIDE], F32, name=f"summed{r}")
+                nc.vector.tensor_tensor(summed[:], adapter[:], term[:], ADD)
+                adapter = summed
+
+        result = held.tile([P, WIDE], F32, name="result")
+        nc.vector.tensor_tensor(result[:], adapter[:], sel[:], MULT)
+        nc.sync.dma_start(out.rearrange("(k t) j -> t k j", t=P), by_block(result[:]))

@@ -1,38 +1,27 @@
 import concourse.mybir as mybir
+from concourse.masks import make_identity
 
 F32, BF16, U16 = mybir.dt.float32, mybir.dt.bfloat16, mybir.dt.uint16
-MULT, ADD, SUBTRACT, MAX = (
-    mybir.AluOpType.mult,
-    mybir.AluOpType.add,
-    mybir.AluOpType.subtract,
-    mybir.AluOpType.max,
-)
+MULT, SUBTRACT = mybir.AluOpType.mult, mybir.AluOpType.subtract
 EXP, COPY = mybir.ActivationFunctionType.Exp, mybir.ActivationFunctionType.Copy
+ALONG_ROW = mybir.AxisListType.X
 
 P = 128
 TOKENS = 128
 RULES = 1024
 RANKS = 4
 BLOCKS = 4
-WIDE = BLOCKS * TOKENS
 
 FLOPS = 2 * (2 * BLOCKS * RANKS * P * TOKENS)
-
-
-def by_block(ap):
-    return ap.rearrange("p (k j) -> p k j", k=BLOCKS)
-
-
-def over_blocks(ap):
-    return ap.unsqueeze(1).to_broadcast([P, BLOCKS, TOKENS])
 
 
 def tile_ruleawareprojection_kernel(tc, xt, rule_in, rule_out_tok, logits_tok, offs, out):
     nc = tc.nc
     with (
         tc.tile_pool(name="held", bufs=1) as held,
-        tc.tile_pool(name="ring", bufs=2) as ring,
-        tc.psum_pool(name="psum", bufs=2) as psum,
+        tc.tile_pool(name="ring", bufs=4) as ring,
+        tc.psum_pool(name="once", bufs=1) as once,
+        tc.psum_pool(name="sums", bufs=2) as sums,
     ):
         offsets = held.tile([P, TOKENS // 16], U16, name="offsets")
         nc.sync.dma_start(offsets[:], offs)
@@ -42,62 +31,69 @@ def tile_ruleawareprojection_kernel(tc, xt, rule_in, rule_out_tok, logits_tok, o
             nc.sync.dma_start(table[:], rule_in[r * P : (r + 1) * P, :])
             tables.append(table)
 
-        x = held.tile([P, WIDE], F32, name="x")
-        nc.scalar.dma_start(by_block(x[:]), xt.rearrange("(k s) j -> s k j", s=P))
-        logits = held.tile([P, WIDE], F32, name="logits")
-        nc.scalar.dma_start(logits[:], logits_tok.rearrange("k j -> (k j)").partition_broadcast(P))
-        factor_out = held.tile([P, RANKS * TOKENS], F32, name="factor_out")
-        nc.scalar.dma_start(
-            factor_out[:].rearrange("t (r j) -> t r j", r=RANKS),
-            rule_out_tok.rearrange("(r t) j -> t r j", t=P),
-        )
+        logits = held.tile([BLOCKS, TOKENS], F32, name="logits")
+        nc.scalar.dma_start(logits[:], logits_tok)
+        x = held.tile([P, BLOCKS, TOKENS], F32, name="x")
+        nc.scalar.dma_start(x[:], xt.rearrange("(k s) j -> s k j", s=P))
+        factor_out = held.tile([P, RANKS, TOKENS], F32, name="factor_out")
+        nc.scalar.dma_start(factor_out[:], rule_out_tok.rearrange("(r t) j -> t r j", t=P))
 
-        ones = held.tile([P, P], BF16, name="ones")
-        nc.gpsimd.memset(ones[:], 1.0)
+        identity = held.tile([P, P], F32, name="identity")
+        make_identity(nc, identity[:])
+        ones = held.tile([P, 1], BF16, name="ones")
+        nc.vector.memset(ones[:], 1.0)
 
-        half = held.tile([P, 2 * TOKENS], F32, name="half")
-        nc.vector.tensor_tensor(half[:], logits[:, : 2 * TOKENS], logits[:, 2 * TOKENS :], MAX)
-        peak = held.tile([P, TOKENS], F32, name="peak")
-        nc.vector.tensor_tensor(peak[:], half[:, :TOKENS], half[:, TOKENS:], MAX)
-        shifted = held.tile([P, WIDE], F32, name="shifted")
-        nc.vector.tensor_tensor(by_block(shifted[:]), by_block(logits[:]), over_blocks(peak[:]), SUBTRACT)
-        weight = held.tile([P, WIDE], F32, name="weight")
+        logits_tok_ps = once.tile([TOKENS, BLOCKS], F32, name="logits_tok_ps")
+        nc.tensor.matmul(logits_tok_ps[:], logits[:], identity[:BLOCKS, :BLOCKS])
+        peak = held.tile([TOKENS, 1], F32, name="peak")
+        nc.vector.reduce_max(peak[:], logits_tok_ps[:], ALONG_ROW)
+        shifted = held.tile([TOKENS, BLOCKS], F32, name="shifted")
+        nc.vector.tensor_scalar(shifted[:], logits_tok_ps[:], peak[:], None, SUBTRACT)
+        weight = held.tile([TOKENS, BLOCKS], F32, name="weight")
         nc.scalar.activation(weight[:], shifted[:], EXP, scale=2.0)
-        half_sum = held.tile([P, 2 * TOKENS], F32, name="half_sum")
-        nc.vector.tensor_tensor(half_sum[:], weight[:, : 2 * TOKENS], weight[:, 2 * TOKENS :], ADD)
-        total = held.tile([P, TOKENS], F32, name="total")
-        nc.vector.tensor_tensor(total[:], half_sum[:, :TOKENS], half_sum[:, TOKENS:], ADD)
-        inverse = held.tile([P, TOKENS], F32, name="inverse")
+        total = held.tile([TOKENS, 1], F32, name="total")
+        nc.vector.reduce_sum(total[:], weight[:], ALONG_ROW)
+        inverse = held.tile([TOKENS, 1], F32, name="inverse")
         nc.vector.reciprocal(inverse[:], total[:])
-        sel = held.tile([P, WIDE], F32, name="sel")
-        nc.vector.tensor_tensor(by_block(sel[:]), by_block(weight[:]), over_blocks(inverse[:]), MULT)
+        sel_tok = held.tile([TOKENS, BLOCKS], F32, name="sel_tok")
+        nc.vector.tensor_scalar(sel_tok[:], weight[:], inverse[:], None, MULT)
 
-        adapter = None
+        factor_tok_ps = once.tile([TOKENS, RANKS, P], F32, name="factor_tok_ps")
         for r in range(RANKS):
-            product = ring.tile([P, WIDE], F32, name="product")
+            nc.tensor.transpose(factor_tok_ps[:, r, :], factor_out[:, r, :], identity[:])
+        factor_tok = held.tile([TOKENS, RANKS, P], F32, name="factor_tok")
+        nc.scalar.activation(factor_tok[:], factor_tok_ps[:], COPY)
+
+        answers = [once.tile([P, TOKENS], F32, name=f"answer{k}") for k in range(BLOCKS)]
+
+        def look_up(r):
+            hidden_ps = sums.tile([TOKENS, BLOCKS], F32, name="hidden_ps")
             for k in range(BLOCKS):
-                cols = slice(k * TOKENS, (k + 1) * TOKENS)
-                nc.vector.tensor_tensor(product[:, cols], tables[r][:].indirect(offsets[:]), x[:, cols], MULT)
-            rounded = ring.tile([P, WIDE], BF16, name="rounded")
-            nc.scalar.activation(rounded[:], product[:], COPY)
+                product = ring.tile([P, TOKENS], F32, name="product")
+                nc.vector.tensor_tensor(product[:], tables[r][:].indirect(offsets[:]), x[:, k, :], MULT)
+                rounded = ring.tile([P, TOKENS], BF16, name="rounded")
+                nc.scalar.activation(rounded[:], product[:], COPY)
+                nc.tensor.matmul(hidden_ps[:, k : k + 1], rounded[:], ones[:])
+            return hidden_ps
 
-            hidden = psum.tile([P, WIDE], F32, name="hidden")
-            nc.tensor.matmul(hidden[:], ones[:], rounded[:])
+        def apply(r, hidden_ps):
+            gain = ring.tile([TOKENS, BLOCKS], F32, name="gain")
+            nc.vector.tensor_tensor(gain[:], hidden_ps[:], sel_tok[:], MULT)
+            for k in range(BLOCKS):
+                scaled = ring.tile([TOKENS, P], F32, name="scaled")
+                nc.scalar.activation(scaled[:], factor_tok[:, r, :], COPY, scale=gain[:, k : k + 1])
+                nc.tensor.matmul(
+                    answers[k][:], scaled[:], identity[:], is_transpose=True, start=(r == 0), stop=(r == RANKS - 1)
+                )
 
-            term = held.tile([P, WIDE], F32, name=f"term{r}")
-            nc.vector.tensor_tensor(
-                by_block(term[:]),
-                by_block(hidden[:]),
-                over_blocks(factor_out[:, r * TOKENS : (r + 1) * TOKENS]),
-                MULT,
-            )
-            if adapter is None:
-                adapter = term
-            else:
-                summed = held.tile([P, WIDE], F32, name=f"summed{r}")
-                nc.vector.tensor_tensor(summed[:], adapter[:], term[:], ADD)
-                adapter = summed
+        hidden_before = look_up(0)
+        for r in range(1, RANKS):
+            hidden_now = look_up(r)
+            apply(r - 1, hidden_before)
+            hidden_before = hidden_now
+        apply(RANKS - 1, hidden_before)
 
-        result = held.tile([P, WIDE], F32, name="result")
-        nc.vector.tensor_tensor(result[:], adapter[:], sel[:], MULT)
-        nc.sync.dma_start(out.rearrange("(k t) j -> t k j", t=P), by_block(result[:]))
+        result = held.tile([P, BLOCKS, TOKENS], F32, name="result")
+        for k in range(BLOCKS):
+            nc.vector.tensor_copy(result[:, k, :], answers[k][:])
+            nc.sync.dma_start(out[k * P : (k + 1) * P, :], result[:, k, :])

@@ -2,7 +2,7 @@ import concourse.mybir as mybir
 from concourse.masks import make_identity
 
 F32, BF16, U16 = mybir.dt.float32, mybir.dt.bfloat16, mybir.dt.uint16
-MULT, SUBTRACT = mybir.AluOpType.mult, mybir.AluOpType.subtract
+MULT, ADD, SUBTRACT = mybir.AluOpType.mult, mybir.AluOpType.add, mybir.AluOpType.subtract
 EXP, COPY = mybir.ActivationFunctionType.Exp, mybir.ActivationFunctionType.Copy
 ALONG_ROW = mybir.AxisListType.X
 
@@ -14,41 +14,45 @@ BLOCKS = 4
 
 FLOPS = 2 * (2 * BLOCKS * RANKS * P * TOKENS)
 
+GAIN_LAG = 4
+SCALE_LAG = GAIN_LAG + 1
+
 
 def tile_ruleawareprojection_kernel(tc, xt, rule_in, rule_out_tok, logits_tok, offs, out):
     nc = tc.nc
     with (
         tc.tile_pool(name="held", bufs=1) as held,
-        tc.tile_pool(name="ring", bufs=4) as ring,
+        tc.tile_pool(name="ahead", bufs=2 * BLOCKS) as ahead,
+        tc.tile_pool(name="ring", bufs=BLOCKS) as ring,
         tc.psum_pool(name="once", bufs=1) as once,
-        tc.psum_pool(name="sums", bufs=2) as sums,
+        tc.psum_pool(name="quad", bufs=4) as quad,
     ):
         offsets = held.tile([P, TOKENS // 16], U16, name="offsets")
         nc.sync.dma_start(offsets[:], offs)
-        tables = []
-        for r in range(RANKS):
-            table = held.tile([P, RULES], F32, name=f"table{r}")
-            nc.sync.dma_start(table[:], rule_in[r * P : (r + 1) * P, :])
-            tables.append(table)
-
-        logits = held.tile([BLOCKS, TOKENS], F32, name="logits")
-        nc.scalar.dma_start(logits[:], logits_tok)
         x = held.tile([P, BLOCKS, TOKENS], F32, name="x")
-        nc.scalar.dma_start(x[:], xt.rearrange("(k s) j -> s k j", s=P))
+        x_dram = xt.rearrange("(k s) j -> s k j", s=P)
+        tables = [held.tile([P, RULES], F32, name=f"table{r}") for r in range(RANKS)]
+        nc.sync.dma_start(x[:, 0:1, :], x_dram[:, 0:1, :])
+        nc.sync.dma_start(tables[0][:], rule_in[0:P, :])
+        nc.sync.dma_start(x[:, 1:, :], x_dram[:, 1:, :])
         factor_out = held.tile([P, RANKS, TOKENS], F32, name="factor_out")
-        nc.scalar.dma_start(factor_out[:], rule_out_tok.rearrange("(r t) j -> t r j", t=P))
+        nc.sync.dma_start(factor_out[:], rule_out_tok.rearrange("(r t) j -> t r j", t=P))
+        for r in range(1, RANKS):
+            nc.sync.dma_start(tables[r][:], rule_in[r * P : (r + 1) * P, :])
+
+        logits = held.tile([TOKENS, BLOCKS], F32, name="logits")
+        with nc.allow_non_contiguous_dma(reason="512 numbers, four to a token"):
+            nc.scalar.dma_start(logits[:], logits_tok.rearrange("k j -> j k"))
 
         identity = held.tile([P, P], F32, name="identity")
         make_identity(nc, identity[:])
         ones = held.tile([P, 1], BF16, name="ones")
-        nc.vector.memset(ones[:], 1.0)
+        nc.gpsimd.memset(ones[:], 1.0)
 
-        logits_tok_ps = once.tile([TOKENS, BLOCKS], F32, name="logits_tok_ps")
-        nc.tensor.matmul(logits_tok_ps[:], logits[:], identity[:BLOCKS, :BLOCKS])
         peak = held.tile([TOKENS, 1], F32, name="peak")
-        nc.vector.reduce_max(peak[:], logits_tok_ps[:], ALONG_ROW)
+        nc.vector.reduce_max(peak[:], logits[:], ALONG_ROW)
         shifted = held.tile([TOKENS, BLOCKS], F32, name="shifted")
-        nc.vector.tensor_scalar(shifted[:], logits_tok_ps[:], peak[:], None, SUBTRACT)
+        nc.vector.tensor_scalar(shifted[:], logits[:], peak[:], None, SUBTRACT)
         weight = held.tile([TOKENS, BLOCKS], F32, name="weight")
         nc.scalar.activation(weight[:], shifted[:], EXP, scale=2.0)
         total = held.tile([TOKENS, 1], F32, name="total")
@@ -58,40 +62,54 @@ def tile_ruleawareprojection_kernel(tc, xt, rule_in, rule_out_tok, logits_tok, o
         sel_tok = held.tile([TOKENS, BLOCKS], F32, name="sel_tok")
         nc.vector.tensor_scalar(sel_tok[:], weight[:], inverse[:], None, MULT)
 
-        factor_tok_ps = once.tile([TOKENS, RANKS, P], F32, name="factor_tok_ps")
-        for r in range(RANKS):
-            nc.tensor.transpose(factor_tok_ps[:, r, :], factor_out[:, r, :], identity[:])
         factor_tok = held.tile([TOKENS, RANKS, P], F32, name="factor_tok")
-        nc.scalar.activation(factor_tok[:], factor_tok_ps[:], COPY)
+        for r in range(RANKS):
+            factor_tok_ps = quad.tile([TOKENS, P], F32, name="factor_tok_ps", tag="bank")
+            nc.tensor.transpose(factor_tok_ps[:], factor_out[:, r, :], identity[:])
+            nc.scalar.activation(factor_tok[:, r, :], factor_tok_ps[:], COPY)
 
         answers = [once.tile([P, TOKENS], F32, name=f"answer{k}") for k in range(BLOCKS)]
+        hidden = []
+        gains = []
+        kept = []
 
-        def look_up(r):
-            hidden_ps = sums.tile([TOKENS, BLOCKS], F32, name="hidden_ps")
-            for k in range(BLOCKS):
-                product = ring.tile([P, TOKENS], F32, name="product")
-                nc.vector.tensor_tensor(product[:], tables[r][:].indirect(offsets[:]), x[:, k, :], MULT)
-                rounded = ring.tile([P, TOKENS], BF16, name="rounded")
-                nc.scalar.activation(rounded[:], product[:], COPY)
-                nc.tensor.matmul(hidden_ps[:, k : k + 1], rounded[:], ones[:])
-            return hidden_ps
+        def look_up(r, k):
+            product = ahead.tile([P, TOKENS], F32, name="product")
+            nc.vector.tensor_tensor(product[:], tables[r][:].indirect(offsets[:]), x[:, k, :], MULT)
+            rounded = ring.tile([P, TOKENS], BF16, name="rounded")
+            nc.scalar.activation(rounded[:], product[:], COPY)
+            hidden_ps = quad.tile([TOKENS, 1], F32, name="hidden_ps", tag="bank")
+            nc.tensor.matmul(hidden_ps[:], rounded[:], ones[:])
+            hidden.append(hidden_ps)
 
-        def apply(r, hidden_ps):
-            gain = ring.tile([TOKENS, BLOCKS], F32, name="gain")
-            nc.vector.tensor_tensor(gain[:], hidden_ps[:], sel_tok[:], MULT)
-            for k in range(BLOCKS):
-                scaled = ring.tile([TOKENS, P], F32, name="scaled")
-                nc.scalar.activation(scaled[:], factor_tok[:, r, :], COPY, scale=gain[:, k : k + 1])
-                nc.tensor.matmul(
-                    answers[k][:], scaled[:], identity[:], is_transpose=True, start=(r == 0), stop=(r == RANKS - 1)
-                )
+        def weigh(r, k):
+            gain = ring.tile([TOKENS, 1], F32, name="gain")
+            nc.scalar.activation(gain[:], hidden[BLOCKS * r + k][:], COPY, scale=sel_tok[:, k : k + 1])
+            gains.append(gain)
 
-        hidden_before = look_up(0)
-        for r in range(1, RANKS):
-            hidden_now = look_up(r)
-            apply(r - 1, hidden_before)
-            hidden_before = hidden_now
-        apply(RANKS - 1, hidden_before)
+        def apply(r, k):
+            gain = gains[BLOCKS * r + k]
+            if r == RANKS - 2:
+                kept.append(held.tile([TOKENS, P], F32, name=f"kept{k}"))
+                nc.scalar.activation(kept[k][:], factor_tok[:, r, :], COPY, scale=gain[:])
+                return
+            scaled = ring.tile([TOKENS, P], F32, name="scaled")
+            if r == RANKS - 1:
+                nc.vector.scalar_tensor_tensor(scaled[:], factor_tok[:, r, :], gain[:], kept[k][:], MULT, ADD)
+            else:
+                nc.scalar.activation(scaled[:], factor_tok[:, r, :], COPY, scale=gain[:])
+            nc.tensor.matmul(
+                answers[k][:], scaled[:], identity[:], is_transpose=True, start=(r == 0), stop=(r == RANKS - 1)
+            )
+
+        steps = [(r, k) for r in range(RANKS) for k in range(BLOCKS)]
+        for i in range(len(steps) + SCALE_LAG):
+            if i < len(steps):
+                look_up(*steps[i])
+            if 0 <= i - GAIN_LAG < len(steps):
+                weigh(*steps[i - GAIN_LAG])
+            if 0 <= i - SCALE_LAG:
+                apply(*steps[i - SCALE_LAG])
 
         result = held.tile([P, BLOCKS, TOKENS], F32, name="result")
         for k in range(BLOCKS):

@@ -113,5 +113,5 @@ def tile_ruleawareprojection_kernel(tc, xt, rule_in, rule_out_tok, logits_tok, o
 
         result = held.tile([P, BLOCKS, TOKENS], F32, name="result")
         for k in range(BLOCKS):
-            nc.vector.tensor_copy(result[:, k, :], answers[k][:])
+            nc.scalar.activation(result[:, k, :], answers[k][:], COPY)
             nc.sync.dma_start(out[k * P : (k + 1) * P, :], result[:, k, :])

@@ -14,9 +14,6 @@ BLOCKS = 4
 
 FLOPS = 2 * (2 * BLOCKS * RANKS * P * TOKENS)
 
-GAIN_LAG = 4
-SCALE_LAG = GAIN_LAG + 1
-
 
 def tile_ruleawareprojection_kernel(tc, xt, rule_in, rule_out_tok, logits_tok, offs, out):
     nc = tc.nc
@@ -102,14 +99,11 @@ def tile_ruleawareprojection_kernel(tc, xt, rule_in, rule_out_tok, logits_tok, o
                 answers[k][:], scaled[:], identity[:], is_transpose=True, start=(r == 0), stop=(r == RANKS - 1)
             )
 
-        steps = [(r, k) for r in range(RANKS) for k in range(BLOCKS)]
-        for i in range(len(steps) + SCALE_LAG):
-            if i < len(steps):
-                look_up(*steps[i])
-            if 0 <= i - GAIN_LAG < len(steps):
-                weigh(*steps[i - GAIN_LAG])
-            if 0 <= i - SCALE_LAG:
-                apply(*steps[i - SCALE_LAG])
+        for r in range(RANKS):
+            for k in range(BLOCKS):
+                look_up(r, k)
+                weigh(r, k)
+                apply(r, k)
 
         result = held.tile([P, BLOCKS, TOKENS], F32, name="result")
         for k in range(BLOCKS):

@@ -6,13 +6,13 @@ MULT, ADD, SUBTRACT = mybir.AluOpType.mult, mybir.AluOpType.add, mybir.AluOpType
 EXP, COPY = mybir.ActivationFunctionType.Exp, mybir.ActivationFunctionType.Copy
 ALONG_ROW = mybir.AxisListType.X
 
-P = 128
+FEATURES = 128
 TOKENS = 128
 RULES = 1024
 RANKS = 4
 BLOCKS = 4
 
-FLOPS = 2 * (2 * BLOCKS * RANKS * P * TOKENS)
+FLOPS = 2 * (2 * BLOCKS * RANKS * FEATURES * TOKENS)
 
 
 def tile_ruleawareprojection_kernel(tc, xt, rule_in, rule_out_tok, logits_tok, offs, out):
@@ -24,26 +24,26 @@ def tile_ruleawareprojection_kernel(tc, xt, rule_in, rule_out_tok, logits_tok, o
         tc.psum_pool(name="once", bufs=1) as once,
         tc.psum_pool(name="quad", bufs=4) as quad,
     ):
-        offsets = held.tile([P, TOKENS // 16], U16, name="offsets")
+        offsets = held.tile([FEATURES, TOKENS // 16], U16, name="offsets")
         nc.sync.dma_start(offsets[:], offs)
-        x = held.tile([P, BLOCKS, TOKENS], F32, name="x")
-        x_dram = xt.rearrange("(k s) j -> s k j", s=P)
-        tables = [held.tile([P, RULES], F32, name=f"table{r}") for r in range(RANKS)]
+        x = held.tile([FEATURES, BLOCKS, TOKENS], F32, name="x")
+        x_dram = xt.rearrange("(k s) j -> s k j", s=FEATURES)
+        tables = [held.tile([FEATURES, RULES], F32, name=f"table{r}") for r in range(RANKS)]
         nc.sync.dma_start(x[:, 0:1, :], x_dram[:, 0:1, :])
-        nc.sync.dma_start(tables[0][:], rule_in[0:P, :])
+        nc.sync.dma_start(tables[0][:], rule_in[0:FEATURES, :])
         nc.sync.dma_start(x[:, 1:, :], x_dram[:, 1:, :])
-        factor_out = held.tile([P, RANKS, TOKENS], F32, name="factor_out")
-        nc.sync.dma_start(factor_out[:], rule_out_tok.rearrange("(r t) j -> t r j", t=P))
+        factor_out = held.tile([FEATURES, RANKS, TOKENS], F32, name="factor_out")
+        nc.sync.dma_start(factor_out[:], rule_out_tok.rearrange("(r t) j -> t r j", t=FEATURES))
         for r in range(1, RANKS):
-            nc.sync.dma_start(tables[r][:], rule_in[r * P : (r + 1) * P, :])
+            nc.sync.dma_start(tables[r][:], rule_in[r * FEATURES : (r + 1) * FEATURES, :])
 
         logits = held.tile([TOKENS, BLOCKS], F32, name="logits")
         with nc.allow_non_contiguous_dma(reason="512 numbers, four to a token"):
             nc.scalar.dma_start(logits[:], logits_tok.rearrange("k j -> j k"))
 
-        identity = held.tile([P, P], F32, name="identity")
+        identity = held.tile([FEATURES, FEATURES], F32, name="identity")
         make_identity(nc, identity[:])
-        ones = held.tile([P, 1], BF16, name="ones")
+        ones = held.tile([FEATURES, 1], BF16, name="ones")
         nc.gpsimd.memset(ones[:], 1.0)
 
         peak = held.tile([TOKENS, 1], F32, name="peak")
@@ -59,53 +59,47 @@ def tile_ruleawareprojection_kernel(tc, xt, rule_in, rule_out_tok, logits_tok, o
         sel_tok = held.tile([TOKENS, BLOCKS], F32, name="sel_tok")
         nc.vector.tensor_scalar(sel_tok[:], weight[:], inverse[:], None, MULT)
 
-        factor_tok = held.tile([TOKENS, RANKS, P], F32, name="factor_tok")
+        factor_tok = held.tile([TOKENS, RANKS, FEATURES], F32, name="factor_tok")
         for r in range(RANKS):
-            factor_tok_ps = quad.tile([TOKENS, P], F32, name="factor_tok_ps", tag="bank")
+            factor_tok_ps = quad.tile([TOKENS, FEATURES], F32, name="factor_tok_ps", tag="bank")
             nc.tensor.transpose(factor_tok_ps[:], factor_out[:, r, :], identity[:])
             nc.scalar.activation(factor_tok[:, r, :], factor_tok_ps[:], COPY)
 
-        answers = [once.tile([P, TOKENS], F32, name=f"answer{k}") for k in range(BLOCKS)]
-        hidden = []
-        gains = []
+        last_factor = []
+        for k in range(BLOCKS):
+            last_factor.append(held.tile([TOKENS, FEATURES], F32, name=f"last_factor{k}"))
+            nc.scalar.activation(last_factor[k][:], factor_tok[:, RANKS - 1, :], COPY, scale=sel_tok[:, k : k + 1])
+
+        answers = [once.tile([FEATURES, TOKENS], F32, name=f"answer{k}") for k in range(BLOCKS)]
         kept = []
-
-        def look_up(r, k):
-            product = ahead.tile([P, TOKENS], F32, name="product")
-            nc.vector.tensor_tensor(product[:], tables[r][:].indirect(offsets[:]), x[:, k, :], MULT)
-            rounded = ring.tile([P, TOKENS], BF16, name="rounded")
-            nc.scalar.activation(rounded[:], product[:], COPY)
-            hidden_ps = quad.tile([TOKENS, 1], F32, name="hidden_ps", tag="bank")
-            nc.tensor.matmul(hidden_ps[:], rounded[:], ones[:])
-            hidden.append(hidden_ps)
-
-        def weigh(r, k):
-            gain = ring.tile([TOKENS, 1], F32, name="gain")
-            nc.scalar.activation(gain[:], hidden[BLOCKS * r + k][:], COPY, scale=sel_tok[:, k : k + 1])
-            gains.append(gain)
-
-        def apply(r, k):
-            gain = gains[BLOCKS * r + k]
-            if r == RANKS - 2:
-                kept.append(held.tile([TOKENS, P], F32, name=f"kept{k}"))
-                nc.scalar.activation(kept[k][:], factor_tok[:, r, :], COPY, scale=gain[:])
-                return
-            scaled = ring.tile([TOKENS, P], F32, name="scaled")
-            if r == RANKS - 1:
-                nc.vector.scalar_tensor_tensor(scaled[:], factor_tok[:, r, :], gain[:], kept[k][:], MULT, ADD)
-            else:
-                nc.scalar.activation(scaled[:], factor_tok[:, r, :], COPY, scale=gain[:])
-            nc.tensor.matmul(
-                answers[k][:], scaled[:], identity[:], is_transpose=True, start=(r == 0), stop=(r == RANKS - 1)
-            )
 
         for r in range(RANKS):
             for k in range(BLOCKS):
-                look_up(r, k)
-                weigh(r, k)
-                apply(r, k)
+                product = ahead.tile([FEATURES, TOKENS], F32, name="product")
+                nc.vector.tensor_tensor(product[:], tables[r][:].indirect(offsets[:]), x[:, k, :], MULT)
+                rounded = ring.tile([FEATURES, TOKENS], BF16, name="rounded")
+                nc.scalar.activation(rounded[:], product[:], COPY)
 
-        result = held.tile([P, BLOCKS, TOKENS], F32, name="result")
+                hidden_ps = quad.tile([TOKENS, 1], F32, name="hidden_ps", tag="bank")
+                nc.tensor.matmul(hidden_ps[:], rounded[:], ones[:])
+
+                if r == RANKS - 1:
+                    scaled = ring.tile([TOKENS, FEATURES], F32, name="scaled")
+                    nc.vector.scalar_tensor_tensor(scaled[:], last_factor[k][:], hidden_ps[:], kept[k][:], MULT, ADD)
+                else:
+                    gain = ring.tile([TOKENS, 1], F32, name="gain")
+                    nc.scalar.activation(gain[:], hidden_ps[:], COPY, scale=sel_tok[:, k : k + 1])
+                    if r == RANKS - 2:
+                        kept.append(held.tile([TOKENS, FEATURES], F32, name=f"kept{k}"))
+                        nc.scalar.activation(kept[k][:], factor_tok[:, r, :], COPY, scale=gain[:])
+                        continue
+                    scaled = ring.tile([TOKENS, FEATURES], F32, name="scaled")
+                    nc.scalar.activation(scaled[:], factor_tok[:, r, :], COPY, scale=gain[:])
+                nc.tensor.matmul(
+                    answers[k][:], scaled[:], identity[:], is_transpose=True, start=(r == 0), stop=(r == RANKS - 1)
+                )
+
+        result = held.tile([FEATURES, BLOCKS, TOKENS], F32, name="result")
         for k in range(BLOCKS):
             nc.scalar.activation(result[:, k, :], answers[k][:], COPY)
-            nc.sync.dma_start(out[k * P : (k + 1) * P, :], result[:, k, :])
+            nc.sync.dma_start(out[k * FEATURES : (k + 1) * FEATURES, :], result[:, k, :])

@@ -33,8 +33,10 @@ def tile_ruleawareprojection_kernel(tc, xt, rule_in, rule_out_tok, logits_tok, o
         nc.sync.dma_start(tables[0][:], rule_in[0:FEATURES, :])
         nc.sync.dma_start(x[:, 1:, :], x_dram[:, 1:, :])
         factor_out = held.tile([FEATURES, RANKS, TOKENS], F32, name="factor_out")
-        nc.sync.dma_start(factor_out[:], rule_out_tok.rearrange("(r t) j -> t r j", t=FEATURES))
+        factor_dram = rule_out_tok.rearrange("(r t) j -> t r j", t=FEATURES)
         for r in range(1, RANKS):
+            upto = r if r < RANKS - 1 else RANKS
+            nc.sync.dma_start(factor_out[:, r - 1 : upto, :], factor_dram[:, r - 1 : upto, :])
             nc.sync.dma_start(tables[r][:], rule_in[r * FEATURES : (r + 1) * FEATURES, :])
 
         logits = held.tile([TOKENS, BLOCKS], F32, name="logits")
@@ -60,25 +62,33 @@ def tile_ruleawareprojection_kernel(tc, xt, rule_in, rule_out_tok, logits_tok, o
         nc.vector.tensor_scalar(sel_tok[:], weight[:], inverse[:], None, MULT)
 
         factor_tok = held.tile([TOKENS, RANKS, FEATURES], F32, name="factor_tok")
-        for r in range(RANKS):
+
+        def turn_factor(r):
             factor_tok_ps = quad.tile([TOKENS, FEATURES], F32, name="factor_tok_ps", tag="bank")
             nc.tensor.transpose(factor_tok_ps[:], factor_out[:, r, :], identity[:])
             nc.scalar.activation(factor_tok[:, r, :], factor_tok_ps[:], COPY)
 
         last_factor = []
-        for k in range(BLOCKS):
-            last_factor.append(held.tile([TOKENS, FEATURES], F32, name=f"last_factor{k}"))
-            nc.scalar.activation(last_factor[k][:], factor_tok[:, RANKS - 1, :], COPY, scale=sel_tok[:, k : k + 1])
 
         answers = [once.tile([FEATURES, TOKENS], F32, name=f"answer{k}") for k in range(BLOCKS)]
         kept = []
 
         for r in range(RANKS):
+            if r < RANKS - 1:
+                turn_factor(r)
+            if r == RANKS - 2:
+                turn_factor(RANKS - 1)
+                for k in range(BLOCKS):
+                    last_factor.append(held.tile([TOKENS, FEATURES], F32, name=f"last_factor{k}"))
+                    nc.scalar.activation(last_factor[k][:], factor_tok[:, RANKS - 1, :], COPY, scale=sel_tok[:, k : k + 1])
             for k in range(BLOCKS):
                 product = ahead.tile([FEATURES, TOKENS], F32, name="product")
                 nc.vector.tensor_tensor(product[:], tables[r][:].indirect(offsets[:]), x[:, k, :], MULT)
                 rounded = ring.tile([FEATURES, TOKENS], BF16, name="rounded")
-                nc.scalar.activation(rounded[:], product[:], COPY)
+                if r >= RANKS - 2:
+                    nc.vector.tensor_copy(rounded[:], product[:])
+                else:
+                    nc.scalar.activation(rounded[:], product[:], COPY)
 
                 hidden_ps = quad.tile([TOKENS, 1], F32, name="hidden_ps", tag="bank")
                 nc.tensor.matmul(hidden_ps[:], rounded[:], ones[:])

@@ -21,6 +21,7 @@ def tile_ruleawareprojection_kernel(tc, xt, rule_in, rule_out_tok, logits_tok, o
         tc.tile_pool(name="held", bufs=1) as held,
         tc.tile_pool(name="ahead", bufs=2 * BLOCKS) as ahead,
         tc.tile_pool(name="ring", bufs=BLOCKS) as ring,
+        tc.tile_pool(name="wide", bufs=2 * BLOCKS) as wide,
         tc.psum_pool(name="once", bufs=1) as once,
         tc.psum_pool(name="quad", bufs=4) as quad,
     ):
@@ -94,7 +95,7 @@ def tile_ruleawareprojection_kernel(tc, xt, rule_in, rule_out_tok, logits_tok, o
                 nc.tensor.matmul(hidden_ps[:], rounded[:], ones[:])
 
                 if r == RANKS - 1:
-                    scaled = ring.tile([TOKENS, FEATURES], F32, name="scaled")
+                    scaled = wide.tile([TOKENS, FEATURES], F32, name="scaled")
                     nc.vector.scalar_tensor_tensor(scaled[:], last_factor[k][:], hidden_ps[:], kept[k][:], MULT, ADD)
                 else:
                     gain = ring.tile([TOKENS, 1], F32, name="gain")
@@ -103,7 +104,7 @@ def tile_ruleawareprojection_kernel(tc, xt, rule_in, rule_out_tok, logits_tok, o
                         kept.append(held.tile([TOKENS, FEATURES], F32, name=f"kept{k}"))
                         nc.scalar.activation(kept[k][:], factor_tok[:, r, :], COPY, scale=gain[:])
                         continue
-                    scaled = ring.tile([TOKENS, FEATURES], F32, name="scaled")
+                    scaled = wide.tile([TOKENS, FEATURES], F32, name="scaled")
                     nc.scalar.activation(scaled[:], factor_tok[:, r, :], COPY, scale=gain[:])
                 nc.tensor.matmul(
                     answers[k][:], scaled[:], identity[:], is_transpose=True, start=(r == 0), stop=(r == RANKS - 1)

@@ -85,10 +85,11 @@ def tile_ruleawareprojection_kernel(tc, xt, rule_in, rule_out_tok, logits_tok, o
             for k in range(BLOCKS):
                 product = ahead.tile([FEATURES, TOKENS], F32, name="product")
                 nc.vector.tensor_tensor(product[:], tables[r][:].indirect(offsets[:]), x[:, k, :], MULT)
-                rounded = ring.tile([FEATURES, TOKENS], BF16, name="rounded")
                 if r >= RANKS - 2:
+                    rounded = wide.tile([FEATURES, TOKENS], BF16, name="rounded_by_vector")
                     nc.vector.tensor_copy(rounded[:], product[:])
                 else:
+                    rounded = ring.tile([FEATURES, TOKENS], BF16, name="rounded")
                     nc.scalar.activation(rounded[:], product[:], COPY)
 
                 hidden_ps = quad.tile([TOKENS, 1], F32, name="hidden_ps", tag="bank")

@@ -2,7 +2,7 @@ import concourse.mybir as mybir
 from concourse.masks import make_identity
 
 F32, BF16, U16 = mybir.dt.float32, mybir.dt.bfloat16, mybir.dt.uint16
-MULT, ADD, SUBTRACT = mybir.AluOpType.mult, mybir.AluOpType.add, mybir.AluOpType.subtract
+MULT, SUBTRACT = mybir.AluOpType.mult, mybir.AluOpType.subtract
 EXP, COPY = mybir.ActivationFunctionType.Exp, mybir.ActivationFunctionType.Copy
 ALONG_ROW = mybir.AxisListType.X
 
@@ -20,7 +20,7 @@ def tile_ruleawareprojection_kernel(tc, xt, rule_in, rule_out_tok, logits_tok, o
     with (
         tc.tile_pool(name="held", bufs=1) as held,
         tc.tile_pool(name="ahead", bufs=2 * BLOCKS) as ahead,
-        tc.tile_pool(name="ring", bufs=BLOCKS) as ring,
+        tc.tile_pool(name="flight", bufs=BLOCKS + 1) as flight,
         tc.tile_pool(name="wide", bufs=2 * BLOCKS) as wide,
         tc.psum_pool(name="once", bufs=1) as once,
         tc.psum_pool(name="quad", bufs=4) as quad,
@@ -54,62 +54,64 @@ def tile_ruleawareprojection_kernel(tc, xt, rule_in, rule_out_tok, logits_tok, o
         shifted = held.tile([TOKENS, BLOCKS], F32, name="shifted")
         nc.vector.tensor_scalar(shifted[:], logits[:], peak[:], None, SUBTRACT)
         weight = held.tile([TOKENS, BLOCKS], F32, name="weight")
-        nc.scalar.activation(weight[:], shifted[:], EXP, scale=2.0)
         total = held.tile([TOKENS, 1], F32, name="total")
-        nc.vector.reduce_sum(total[:], weight[:], ALONG_ROW)
+        nc.scalar.activation(weight[:], shifted[:], EXP, scale=2.0, accum_out=total[:])
         inverse = held.tile([TOKENS, 1], F32, name="inverse")
         nc.vector.reciprocal(inverse[:], total[:])
-        sel_tok = held.tile([TOKENS, BLOCKS], F32, name="sel_tok")
-        nc.vector.tensor_scalar(sel_tok[:], weight[:], inverse[:], None, MULT)
 
         factor_tok = held.tile([TOKENS, RANKS, FEATURES], F32, name="factor_tok")
 
         def turn_factor(r):
             factor_tok_ps = quad.tile([TOKENS, FEATURES], F32, name="factor_tok_ps", tag="bank")
             nc.tensor.transpose(factor_tok_ps[:], factor_out[:, r, :], identity[:])
-            nc.scalar.activation(factor_tok[:, r, :], factor_tok_ps[:], COPY)
-
-        last_factor = []
+            nc.scalar.activation(factor_tok[:, r, :], factor_tok_ps[:], COPY, scale=inverse[:])
 
         answers = [once.tile([FEATURES, TOKENS], F32, name=f"answer{k}") for k in range(BLOCKS)]
-        kept = []
 
+        def look_up(r, k):
+            product = ahead.tile([FEATURES, TOKENS], F32, name="product")
+            nc.vector.tensor_tensor(product[:], tables[r][:].indirect(offsets[:]), x[:, k, :], MULT)
+            return product
+
+        def add_up(r, k, product):
+            if r == RANKS - 1:
+                rounded = wide.tile([FEATURES, TOKENS], BF16, name="rounded_by_vector")
+                nc.vector.tensor_copy(rounded[:], product[:])
+            else:
+                rounded = flight.tile([FEATURES, TOKENS], BF16, name="rounded", tag="step")
+                nc.scalar.activation(rounded[:], product[:], COPY)
+
+            hidden_ps = quad.tile([TOKENS, 1], F32, name="hidden_ps", tag="bank")
+            nc.tensor.matmul(hidden_ps[:], rounded[:], ones[:])
+            return hidden_ps
+
+        def use(r, k, hidden_ps):
+            if r == RANKS - 1:
+                scaled = wide.tile([TOKENS, FEATURES], F32, name="scaled_by_vector")
+                nc.vector.tensor_scalar(scaled[:], factor_tok[:, r, :], hidden_ps[:], weight[:, k : k + 1], MULT, MULT)
+            else:
+                gain = flight.tile([TOKENS, 1], F32, name="gain", tag="step")
+                nc.scalar.activation(gain[:], hidden_ps[:], COPY, scale=weight[:, k : k + 1])
+                scaled = wide.tile([TOKENS, FEATURES], F32, name="scaled")
+                nc.scalar.activation(scaled[:], factor_tok[:, r, :], COPY, scale=gain[:])
+            nc.tensor.matmul(
+                answers[k][:], scaled[:], identity[:], is_transpose=True, start=(r == 0), stop=(r == RANKS - 1)
+            )
+
+        LAG = 2
+        waiting = []
         for r in range(RANKS):
             if r < RANKS - 1:
                 turn_factor(r)
             if r == RANKS - 2:
                 turn_factor(RANKS - 1)
-                for k in range(BLOCKS):
-                    last_factor.append(held.tile([TOKENS, FEATURES], F32, name=f"last_factor{k}"))
-                    nc.scalar.activation(last_factor[k][:], factor_tok[:, RANKS - 1, :], COPY, scale=sel_tok[:, k : k + 1])
             for k in range(BLOCKS):
-                product = ahead.tile([FEATURES, TOKENS], F32, name="product")
-                nc.vector.tensor_tensor(product[:], tables[r][:].indirect(offsets[:]), x[:, k, :], MULT)
-                if r >= RANKS - 2:
-                    rounded = wide.tile([FEATURES, TOKENS], BF16, name="rounded_by_vector")
-                    nc.vector.tensor_copy(rounded[:], product[:])
-                else:
-                    rounded = ring.tile([FEATURES, TOKENS], BF16, name="rounded")
-                    nc.scalar.activation(rounded[:], product[:], COPY)
-
-                hidden_ps = quad.tile([TOKENS, 1], F32, name="hidden_ps", tag="bank")
-                nc.tensor.matmul(hidden_ps[:], rounded[:], ones[:])
-
-                if r == RANKS - 1:
-                    scaled = wide.tile([TOKENS, FEATURES], F32, name="scaled")
-                    nc.vector.scalar_tensor_tensor(scaled[:], last_factor[k][:], hidden_ps[:], kept[k][:], MULT, ADD)
-                else:
-                    gain = ring.tile([TOKENS, 1], F32, name="gain")
-                    nc.scalar.activation(gain[:], hidden_ps[:], COPY, scale=sel_tok[:, k : k + 1])
-                    if r == RANKS - 2:
-                        kept.append(held.tile([TOKENS, FEATURES], F32, name=f"kept{k}"))
-                        nc.scalar.activation(kept[k][:], factor_tok[:, r, :], COPY, scale=gain[:])
-                        continue
-                    scaled = wide.tile([TOKENS, FEATURES], F32, name="scaled")
-                    nc.scalar.activation(scaled[:], factor_tok[:, r, :], COPY, scale=gain[:])
-                nc.tensor.matmul(
-                    answers[k][:], scaled[:], identity[:], is_transpose=True, start=(r == 0), stop=(r == RANKS - 1)
-                )
+                waiting.append((r, k, add_up(r, k, look_up(r, k))))
+                if len(waiting) > LAG:
+                    use(*waiting[0])
+                    waiting = waiting[1:]
+        for step in waiting:
+            use(*step)
 
         result = held.tile([FEATURES, BLOCKS, TOKENS], F32, name="result")
         for k in range(BLOCKS):

@@ -99,6 +99,7 @@ def tile_ruleawareprojection_kernel(tc, xt, rule_in, rule_out_tok, logits_tok, o
             )
 
         LAG = 2
+        products = []
         waiting = []
         for r in range(RANKS):
             if r < RANKS - 1:
@@ -106,10 +107,14 @@ def tile_ruleawareprojection_kernel(tc, xt, rule_in, rule_out_tok, logits_tok, o
             if r == RANKS - 2:
                 turn_factor(RANKS - 1)
             for k in range(BLOCKS):
-                waiting.append((r, k, add_up(r, k, look_up(r, k))))
+                products.append((r, k, look_up(r, k)))
+                if len(products) > (1 if r == RANKS - 1 else 0):
+                    waiting.append((*products[0][:2], add_up(*products[0])))
+                    products = products[1:]
                 if len(waiting) > LAG:
                     use(*waiting[0])
                     waiting = waiting[1:]
+        waiting.append((*products[0][:2], add_up(*products[0])))
         for step in waiting:
             use(*step)
 

import concourse.mybir as mybir
from concourse.masks import make_identity

F32, BF16, U16 = mybir.dt.float32, mybir.dt.bfloat16, mybir.dt.uint16
MULT, SUBTRACT = mybir.AluOpType.mult, mybir.AluOpType.subtract
EXP, COPY = mybir.ActivationFunctionType.Exp, mybir.ActivationFunctionType.Copy
ALONG_ROW = mybir.AxisListType.X

FEATURES = 128
TOKENS = 128
RULES = 1024
RANKS = 4
BLOCKS = 4

FLOPS = 2 * (2 * BLOCKS * RANKS * FEATURES * TOKENS)


def tile_ruleawareprojection_kernel(tc, xt, rule_in, rule_out_tok, logits_tok, offs, out):
    nc = tc.nc
    with (
        tc.tile_pool(name="held", bufs=1) as held,
        tc.tile_pool(name="ahead", bufs=2 * BLOCKS) as ahead,
        tc.tile_pool(name="flight", bufs=BLOCKS + 1) as flight,
        tc.tile_pool(name="wide", bufs=2 * BLOCKS) as wide,
        tc.psum_pool(name="once", bufs=1) as once,
        tc.psum_pool(name="quad", bufs=4) as quad,
    ):
        offsets = held.tile([FEATURES, TOKENS // 16], U16, name="offsets")
        nc.sync.dma_start(offsets[:], offs)
        x = held.tile([FEATURES, BLOCKS, TOKENS], F32, name="x")
        x_dram = xt.rearrange("(k s) j -> s k j", s=FEATURES)
        tables = [held.tile([FEATURES, RULES], F32, name=f"table{r}") for r in range(RANKS)]
        nc.sync.dma_start(x[:, 0:1, :], x_dram[:, 0:1, :])
        nc.sync.dma_start(tables[0][:], rule_in[0:FEATURES, :])
        nc.sync.dma_start(x[:, 1:, :], x_dram[:, 1:, :])
        factor_out = held.tile([FEATURES, RANKS, TOKENS], F32, name="factor_out")
        factor_dram = rule_out_tok.rearrange("(r t) j -> t r j", t=FEATURES)
        for r in range(1, RANKS):
            upto = r if r < RANKS - 1 else RANKS
            nc.sync.dma_start(factor_out[:, r - 1 : upto, :], factor_dram[:, r - 1 : upto, :])
            nc.sync.dma_start(tables[r][:], rule_in[r * FEATURES : (r + 1) * FEATURES, :])

        logits = held.tile([TOKENS, BLOCKS], F32, name="logits")
        with nc.allow_non_contiguous_dma(reason="512 numbers, four to a token"):
            nc.scalar.dma_start(logits[:], logits_tok.rearrange("k j -> j k"))

        identity = held.tile([FEATURES, FEATURES], F32, name="identity")
        make_identity(nc, identity[:])
        ones = held.tile([FEATURES, 1], BF16, name="ones")
        nc.gpsimd.memset(ones[:], 1.0)

        peak = held.tile([TOKENS, 1], F32, name="peak")
        nc.vector.reduce_max(peak[:], logits[:], ALONG_ROW)
        shifted = held.tile([TOKENS, BLOCKS], F32, name="shifted")
        nc.vector.tensor_scalar(shifted[:], logits[:], peak[:], None, SUBTRACT)
        weight = held.tile([TOKENS, BLOCKS], F32, name="weight")
        total = held.tile([TOKENS, 1], F32, name="total")
        nc.scalar.activation(weight[:], shifted[:], EXP, scale=2.0, accum_out=total[:])
        inverse = held.tile([TOKENS, 1], F32, name="inverse")
        nc.vector.reciprocal(inverse[:], total[:])

        factor_tok = held.tile([TOKENS, RANKS, FEATURES], F32, name="factor_tok")

        def turn_factor(r):
            factor_tok_ps = quad.tile([TOKENS, FEATURES], F32, name="factor_tok_ps", tag="bank")
            nc.tensor.transpose(factor_tok_ps[:], factor_out[:, r, :], identity[:])
            nc.scalar.activation(factor_tok[:, r, :], factor_tok_ps[:], COPY, scale=inverse[:])

        answers = [once.tile([FEATURES, TOKENS], F32, name=f"answer{k}") for k in range(BLOCKS)]

        def look_up(r, k):
            product = ahead.tile([FEATURES, TOKENS], F32, name="product")
            nc.vector.tensor_tensor(product[:], tables[r][:].indirect(offsets[:]), x[:, k, :], MULT)
            return product

        def add_up(r, k, product):
            if r == RANKS - 1:
                rounded = wide.tile([FEATURES, TOKENS], BF16, name="rounded_by_vector")
                nc.vector.tensor_copy(rounded[:], product[:])
            else:
                rounded = flight.tile([FEATURES, TOKENS], BF16, name="rounded", tag="step")
                nc.scalar.activation(rounded[:], product[:], COPY)

            hidden_ps = quad.tile([TOKENS, 1], F32, name="hidden_ps", tag="bank")
            nc.tensor.matmul(hidden_ps[:], rounded[:], ones[:])
            return hidden_ps

        def use(r, k, hidden_ps):
            if r == RANKS - 1:
                scaled = wide.tile([TOKENS, FEATURES], F32, name="scaled_by_vector")
                nc.vector.tensor_scalar(scaled[:], factor_tok[:, r, :], hidden_ps[:], weight[:, k : k + 1], MULT, MULT)
            else:
                gain = flight.tile([TOKENS, 1], F32, name="gain", tag="step")
                nc.scalar.activation(gain[:], hidden_ps[:], COPY, scale=weight[:, k : k + 1])
                scaled = wide.tile([TOKENS, FEATURES], F32, name="scaled")
                nc.scalar.activation(scaled[:], factor_tok[:, r, :], COPY, scale=gain[:])
            nc.tensor.matmul(
                answers[k][:], scaled[:], identity[:], is_transpose=True, start=(r == 0), stop=(r == RANKS - 1)
            )

        LAG = 2
        products = []
        waiting = []
        for r in range(RANKS):
            if r < RANKS - 1:
                turn_factor(r)
            if r == RANKS - 2:
                turn_factor(RANKS - 1)
            for k in range(BLOCKS):
                products.append((r, k, look_up(r, k)))
                if len(products) > (1 if r == RANKS - 1 else 0):
                    waiting.append((*products[0][:2], add_up(*products[0])))
                    products = products[1:]
                if len(waiting) > LAG:
                    use(*waiting[0])
                    waiting = waiting[1:]
        waiting.append((*products[0][:2], add_up(*products[0])))
        for step in waiting:
            use(*step)

        result = held.tile([FEATURES, BLOCKS, TOKENS], F32, name="result")
        for k in range(BLOCKS):
            nc.scalar.activation(result[:, k, :], answers[k][:], COPY)
            nc.sync.dma_start(out[k * FEATURES : (k + 1) * FEATURES, :], result[:, k, :])
